import numpy as np
import ml_dtypes


def mxq(x, axis, fmt="e4m3"):
    dtype, down = {"e4m3": (ml_dtypes.float8_e4m3fn, 7), "e5m2": (ml_dtypes.float8_e5m2, 14)}[fmt]
    v = np.moveaxis(np.asarray(x, np.float32).astype(ml_dtypes.bfloat16).astype(np.float64), axis, -1)
    blocks = v.reshape(v.shape[:-1] + (-1, 32))
    amax = np.abs(blocks).max(-1, keepdims=True)
    byte = np.maximum(np.where(amax > 0, np.frexp(amax)[1] - 1 + 127, 0) - down, 1)
    scale = np.exp2(byte - 127.0)
    codes = (blocks / scale).astype(np.float32).astype(dtype).astype(np.float64)
    return np.moveaxis((codes * scale).reshape(v.shape), -1, axis)


WIDE = False


def mx_kscale(k):
    if not WIDE:
        return np.ones(k)
    levels = np.array([10, -10, 5, -5, 0])
    if k % 512:
        return np.exp2(np.random.permutation(np.resize(levels, k // 32))).repeat(32)
    a = np.empty((k // 512, 16))
    for p in range(k // 512):
        a[p, :8] = np.random.permutation(np.resize(levels, 8))
        for g in range(8):
            far = levels[np.abs(levels - a[p, g]) >= 10]
            a[p, g + 8] = far[np.random.randint(len(far))]
    return np.exp2(a.ravel()).repeat(32)


BF16 = ml_dtypes.bfloat16


def bf(x):
    return np.asarray(x, np.float32).astype(BF16)


def f64(x):
    return np.asarray(x).astype(np.float64)


B, D, DO, H, T, P = 1024, 1024, 1024, 256, 8, 2


def setup_inputs():
    s = mx_kscale(D)
    return {"transformed": bf(np.random.standard_normal((B, D)) * 1.8 * s),
            "coeff": bf(np.random.standard_normal(B) * 0.45),
            "task_mat": bf(np.random.standard_normal((D, D)) / np.sqrt(D) / s[:, None] * s[None, :]),
            "Wp": bf(np.random.standard_normal((DO, D)) / np.sqrt(D) / s[None, :])}


def reference(transformed, coeff, task_mat, Wp):
    x = f64(transformed)
    y = x + f64(coeff)[:, None] * (mxq(x, 1, "e4m3") @ mxq(f64(task_mat), 0, "e4m3"))
    return mxq(y, 1, "e4m3") @ mxq(f64(Wp), 1, "e4m3").T

@@ -1,0 +1,246 @@
+from contextlib import ExitStack
+
+import concourse.mybir as mybir
+from concourse.masks import make_identity
+
+F32 = mybir.dt.float32
+BF16 = mybir.dt.bfloat16
+U32 = mybir.dt.uint32
+U8 = mybir.dt.uint8
+FP8X4 = mybir.dt.float8_e4m3fn_x4
+MULT = mybir.AluOpType.mult
+ADD = mybir.AluOpType.add
+
+P = 128
+FLOPS = 2 * 2 * 1024 * 1024 * 1024
+VCOLS = 352
+
+ORDER = [
+    ("LT", 0, 0), ("LC",), ("LT", 0, 1), ("CT",), ("LX", 0),
+    ("CC",), ("LT", 1, 0), ("LT", 1, 1), ("RV", 0, 0), ("RS", 0, 0),
+    ("XT", 0), ("RS", 0, 1), ("LX", 1), ("RV", 0, 1), ("LX", 2),
+    ("XC", 0, "S"), ("QT", 0, 0), ("LX", 3), ("QT", 0, 1), ("LX", 4),
+    ("RS", 1, 0), ("XQ", 0), ("LX", 5), ("RV", 1, 0), ("XT", 1),
+    ("RS", 1, 1), ("LW", 0), ("S1", 0, 0, 0), ("QT", 1, 0), ("S1", 0, 1, 0),
+    ("XC", 1, "S"), ("XT", 2), ("RV", 1, 1), ("XT", 3), ("XC", 2, "S"),
+    ("XT", 4), ("QT", 1, 1), ("XT", 5), ("XC", 3, "S"), ("LX", 6),
+    ("S1", 0, 0, 1), ("XQ", 1), ("XC", 4, "S"), ("XQ", 2), ("S1", 0, 1, 1),
+    ("LX", 7), ("E", 0, 0), ("S1", 1, 0, 0), ("S1", 1, 0, 1), ("XC", 5, "S"),
+    ("LW", 1), ("S1", 1, 1, 0), ("E", 0, 1), ("S1", 1, 1, 1), ("S1", 2, 0, 0),
+    ("E", 1, 0), ("S1", 2, 0, 1), ("S1", 2, 1, 0), ("E", 1, 1), ("S1", 2, 1, 1),
+    ("WT", 0), ("E", 2, 0), ("YT", 0), ("WC", 0, "S"), ("E", 2, 1),
+    ("WT", 1), ("YT", 1), ("YC", 0, "S"), ("XQ", 3), ("XQ", 4),
+    ("WT", 2), ("XQ", 5), ("YT", 2), ("WC", 1, "V"), ("YC", 1, "S"),
+    ("WT", 3), ("YQ", 0), ("WT", 4), ("WC", 2, "V"), ("WT", 5),
+    ("YC", 2, "S"), ("WT", 6), ("YQ", 1), ("XT", 6), ("WC", 3, "V"),
+    ("WT", 7), ("XT", 7), ("WC", 4, "S"), ("WQ", 0, 0), ("S1", 3, 0, 0),
+    ("S1", 3, 0, 1), ("WQ", 0, 1), ("WC", 5, "S"), ("S1", 3, 1, 0), ("S1", 3, 1, 1),
+    ("YQ", 2), ("WC", 6, "S"), ("S1", 4, 0, 0), ("E", 3, 0), ("S2", 0, 0),
+    ("XC", 6, "S"), ("E", 3, 1), ("S2", 1, 0), ("WC", 7, "S"), ("XQ", 6),
+    ("S2", 2, 0), ("XC", 7, "V"), ("OC", 0, 0, "S"), ("S1", 4, 0, 1), ("WQ", 1, 0),
+    ("S1", 4, 1, 0), ("OC", 1, 0, "S"), ("ST", 0, 0), ("S1", 4, 1, 1), ("S1", 5, 0, 0),
+    ("WQ", 1, 1), ("OC", 2, 0, "S"), ("ST", 1, 0), ("S1", 5, 0, 1), ("S1", 5, 1, 0),
+    ("E", 4, 0), ("S1", 5, 1, 1), ("ST", 2, 0), ("S2", 0, 1), ("E", 4, 1),
+    ("S2", 1, 1), ("E", 5, 0), ("OC", 0, 1, "S"), ("S2", 2, 1), ("E", 5, 1),
+    ("OC", 1, 1, "S"), ("ST", 0, 1), ("S1", 6, 0, 0), ("XQ", 7), ("S1", 6, 0, 1),
+    ("OC", 2, 1, "S"), ("ST", 1, 1), ("S1", 6, 1, 0), ("E", 6, 0), ("S1", 6, 1, 1),
+    ("S1", 7, 0, 0), ("ST", 2, 1), ("S1", 7, 0, 1), ("E", 6, 1), ("S1", 7, 1, 0),
+    ("S1", 7, 1, 1), ("E", 7, 0), ("YT", 3), ("E", 7, 1), ("YT", 4),
+    ("YC", 3, "S"), ("YT", 5), ("YC", 4, "V"), ("YT", 6), ("YC", 5, "S"),
+    ("YT", 7), ("YQ", 3), ("YQ", 4), ("YC", 7, "V"), ("S2", 3, 0),
+    ("YC", 6, "S"), ("S2", 3, 1), ("YQ", 5), ("OC", 3, 0, "S"), ("S2", 4, 0),
+    ("YQ", 6), ("YQ", 7), ("OC", 3, 1, "S"), ("S2", 4, 1), ("ST", 3, 0),
+    ("OC", 4, 0, "V"), ("S2", 5, 0), ("ST", 3, 1), ("OC", 4, 1, "S"), ("S2", 5, 1),
+    ("ST", 4, 0), ("OC", 5, 0, "S"), ("S2", 6, 0), ("ST", 4, 1), ("OC", 5, 1, "V"),
+    ("S2", 6, 1), ("ST", 5, 0), ("OC", 6, 0, "S"), ("S2", 7, 0), ("ST", 5, 1),
+    ("OC", 6, 1, "S"), ("S2", 7, 1), ("ST", 6, 0), ("OC", 7, 0, "V"), ("ST", 6, 1),
+    ("OC", 7, 1, "S"), ("ST", 7, 0), ("ST", 7, 1),
+]
+
+
+def tile_precomputedmetanet_pb_kernel(tc, transformed, coeff, task_mat, Wp, out):
+    nc = tc.nc
+    with ExitStack() as ctx:
+        keep = ctx.enter_context(tc.tile_pool(name="keep", bufs=1))
+        psum = ctx.enter_context(tc.psum_pool(name="psum", bufs=8))
+        ctx.enter_context(tc.manual_schedule())
+
+        ident_b = keep.tile([P, P], BF16, name="ident_b")
+        ident_f = keep.tile([P, P], F32, name="ident_f")
+        crow = keep.tile([P, P], BF16, name="crow")
+        c_sb = keep.tile([P, 8], F32, name="c_sb")
+        nc.vector.memset(crow[:], 0.0)
+        make_identity(nc, ident_b[:])
+        make_identity(nc, ident_f[:])
+
+        traw = keep.tile([P, 2, 4, 1024], BF16, name="traw")
+        tcod = keep.tile([P, 2, 1024], U32, name="tcod", align_bytes=64)
+        tscl = keep.tile([P, 2, 1024], U8, name="tscl", align_bytes=64)
+        wraw = keep.tile([P, 8, 1024], BF16, name="wraw")
+        wcod = keep.tile([P, 2, 1024], U32, name="wcod", align_bytes=64)
+        wscl = keep.tile([P, 2, 1024], U8, name="wscl", align_bytes=64)
+        tgrp = {}
+        for g in range(2):
+            for c in range(2):
+                tgrp[(g, c)] = keep.tile([P, 512, 4], BF16, name="tgrp%d%d" % (g, c), align_bytes=64)
+        wgrp = [keep.tile([P, 2, 2048], BF16, name="wgrp%d" % c, align_bytes=64) for c in range(2)]
+        x_sb = [keep.tile([P, 1024], BF16, name="x_sb%d" % i) for i in range(8)]
+        xgrp = [keep.tile([P, 1024], BF16, name="xgrp%d" % i, align_bytes=64) for i in range(8)]
+        xcod = [keep.tile([P, 256], U32, name="xcod%d" % i, align_bytes=64) for i in range(8)]
+        xscl = [keep.tile([P, 256], U8, name="xscl%d" % i, align_bytes=64) for i in range(8)]
+        y_sb = [keep.tile([P, 4, 256], BF16, name="y_sb%d" % i) for i in range(8)]
+        ygrp = [keep.tile([P, 1024], BF16, name="ygrp%d" % i, align_bytes=64) for i in range(8)]
+        ycod = [keep.tile([P, 256], U32, name="ycod%d" % i, align_bytes=64) for i in range(8)]
+        yscl = [keep.tile([P, 256], U8, name="yscl%d" % i, align_bytes=64) for i in range(8)]
+        obuf = [keep.tile([P, 1024], F32, name="obuf%d" % i) for i in range(8)]
+        bank = {}
+
+        def copy(eng, dst, src):
+            if eng == "V":
+                nc.vector.tensor_copy(out=dst, in_=src)
+            else:
+                nc.scalar.copy(out=dst, in_=src)
+
+        def new_bank(key, shape, dtype):
+            t = psum.tile(shape, dtype, name="ps", tag="ps")
+            bank[key] = t
+            return t
+
+        def op_lc():
+            nc.scalar.dma_start(out=crow[0:8, :], in_=coeff.rearrange("(i p) -> i p", p=P))
+
+        def op_lt(g, u):
+            rows = task_mat[512 * g : 512 * g + 512, :].rearrange("(p t) d -> p t d", t=4)
+            nc.sync.dma_start(out=traw[:, g, 2 * u : 2 * u + 2, :], in_=rows[:, 2 * u : 2 * u + 2, :])
+
+        def op_lx(i):
+            nc.sync.dma_start(out=x_sb[i][:], in_=transformed[P * i : P * i + P, :])
+
+        def op_lw(c):
+            nc.sync.dma_start(
+                out=wraw[:, 4 * c : 4 * c + 4, :],
+                in_=Wp[512 * c : 512 * c + 512, :].rearrange("(j p) d -> p j d", p=P),
+            )
+
+        def op_ct():
+            t = new_bank("c", [P, P], BF16)
+            nc.tensor.transpose(t[:], crow[:], ident_b[:])
+
+        def op_cc():
+            nc.vector.tensor_copy(out=c_sb[:], in_=bank["c"][:, 0:8])
+
+        def regroup(eng, g, c, lo, hi):
+            src = traw[:, g, :, 512 * c + lo : 512 * c + hi].rearrange("p t (c i) -> p c t i", i=4)
+            dst = tgrp[(g, c)][:, lo:hi, :].rearrange("p (c i) t -> p c t i", i=4)
+            copy(eng, dst, src)
+
+        def op_rv(g, c):
+            regroup("V", g, c, 0, VCOLS)
+
+        def op_rs(g, c):
+            regroup("S", g, c, VCOLS, 512)
+
+        def op_qt(g, c):
+            nc.vector.quantize_mx(
+                out=tcod[:, g, 512 * c : 512 * c + 512].bitcast(FP8X4),
+                scales=tscl[:, g, 512 * c : 512 * c + 512],
+                in_=tgrp[(g, c)][:].rearrange("p d t -> p (d t)"),
+            )
+
+        def word_transposes(key, rows):
+            t = new_bank(key, [P, 4, P], F32)
+            words = rows.bitcast(F32)
+            for q in range(4):
+                lo = 256 * (q // 2) + q % 2
+                nc.tensor.transpose(t[:, q, :], words[:, lo : 256 * (q // 2) + 256 : 2], ident_f[:])
+
+        def op_xt(i):
+            word_transposes(("x", i), x_sb[i][:])
+
+        def op_xc(i, eng):
+            dst = xgrp[i][:].bitcast(F32).rearrange("p (g b u) -> p g b u", g=2, b=P, u=2)
+            copy(eng, dst, bank[("x", i)][:].rearrange("p (g u) b -> p g b u", g=2, u=2))
+
+        def op_xq(i):
+            nc.vector.quantize_mx(out=xcod[i][:].bitcast(FP8X4), scales=xscl[i][:], in_=xgrp[i][:])
+
+        def op_s1(i, c, g):
+            if g == 0:
+                new_bank(("z", i, c), [P, 512], F32)
+            nc.tensor.matmul_mx(
+                out=bank[("z", i, c)][:],
+                lhsT=xcod[i][:, P * g : P * g + P].bitcast(FP8X4),
+                lhsT_scale=xscl[i][:, P * g : P * g + P],
+                rhs=tcod[:, g, 512 * c : 512 * c + 512].bitcast(FP8X4),
+                rhs_scale=tscl[:, g, 512 * c : 512 * c + 512],
+                start=(g == 0),
+                stop=(g == 1),
+            )
+
+        def op_e(i, c):
+            nc.vector.scalar_tensor_tensor(
+                out=y_sb[i][:, :, 128 * c : 128 * c + 128],
+                in0=bank[("z", i, c)][:].rearrange("p (w t) -> p t w", t=4),
+                scalar=c_sb[:, i : i + 1],
+                in1=x_sb[i][:, 512 * c : 512 * c + 512].rearrange("p (w t) -> p t w", t=4),
+                op0=MULT,
+                op1=ADD,
+            )
+
+        def op_yt(i):
+            t = new_bank(("y", i), [P, 8, P], BF16)
+            for g in range(2):
+                for k in range(4):
+                    nc.tensor.transpose(t[:, 4 * g + k, :], y_sb[i][:, k, P * g : P * g + P], ident_b[:])
+
+        def op_yc(i, eng):
+            dst = ygrp[i][:].rearrange("p (g b t) -> p g b t", g=2, b=P, t=4)
+            copy(eng, dst, bank[("y", i)][:].rearrange("p (g t) b -> p g b t", g=2, t=4))
+
+        def op_yq(i):
+            nc.vector.quantize_mx(out=ycod[i][:].bitcast(FP8X4), scales=yscl[i][:], in_=ygrp[i][:])
+
+        def op_wt(j):
+            word_transposes(("w", j), wraw[:, j, :])
+
+        def op_wc(j, eng):
+            lo = P * (j % 4)
+            dst = wgrp[j // 4][:].bitcast(F32).rearrange("p g (o u) -> p g o u", u=2)[:, :, lo : lo + P, :]
+            copy(eng, dst, bank[("w", j)][:].rearrange("p (g u) o -> p g o u", g=2, u=2))
+
+        def op_wq(c, g):
+            nc.vector.quantize_mx(
+                out=wcod[:, g, 512 * c : 512 * c + 512].bitcast(FP8X4),
+                scales=wscl[:, g, 512 * c : 512 * c + 512],
+                in_=wgrp[c][:, g, :],
+            )
+
+        def op_s2(i, c):
+            t = new_bank(("o", i, c), [P, 512], F32)
+            for g in range(2):
+                nc.tensor.matmul_mx(
+                    out=t[:],
+                    lhsT=ycod[i][:, P * g : P * g + P].bitcast(FP8X4),
+                    lhsT_scale=yscl[i][:, P * g : P * g + P],
+                    rhs=wcod[:, g, 512 * c : 512 * c + 512].bitcast(FP8X4),
+                    rhs_scale=wscl[:, g, 512 * c : 512 * c + 512],
+                    start=(g == 0),
+                    stop=(g == 1),
+                )
+
+        def op_oc(i, c, eng):
+            copy(eng, obuf[i][:, 512 * c : 512 * c + 512], bank[("o", i, c)][:])
+
+        def op_st(i, c):
+            nc.sync.dma_start(
+                out=out[P * i : P * i + P, 512 * c : 512 * c + 512], in_=obuf[i][:, 512 * c : 512 * c + 512]
+            )
+
+        ops = {
+            "LC": op_lc, "LT": op_lt, "LX": op_lx, "LW": op_lw, "CT": op_ct, "CC": op_cc,
+            "RV": op_rv, "RS": op_rs, "QT": op_qt, "XT": op_xt, "XC": op_xc, "XQ": op_xq,
+            "S1": op_s1, "E": op_e, "YT": op_yt, "YC": op_yc, "YQ": op_yq,
+            "WT": op_wt, "WC": op_wc, "WQ": op_wq, "S2": op_s2, "OC": op_oc, "ST": op_st,
+        }
+        for step in ORDER:
+            ops[step[0]](*step[1:])

@@ -10,52 +10,12 @@ U8 = mybir.dt.uint8
 FP8X4 = mybir.dt.float8_e4m3fn_x4
 MULT = mybir.AluOpType.mult
 ADD = mybir.AluOpType.add
+COPY = mybir.ActivationFunctionType.Copy
 
 P = 128
 FLOPS = 2 * 2 * 1024 * 1024 * 1024
-VCOLS = 352
-
-ORDER = [
-    ("LT", 0, 0), ("LC",), ("LT", 0, 1), ("CT",), ("LX", 0),
-    ("CC",), ("LT", 1, 0), ("LT", 1, 1), ("RV", 0, 0), ("RS", 0, 0),
-    ("XT", 0), ("RS", 0, 1), ("LX", 1), ("RV", 0, 1), ("LX", 2),
-    ("XC", 0, "S"), ("QT", 0, 0), ("LX", 3), ("QT", 0, 1), ("LX", 4),
-    ("RS", 1, 0), ("XQ", 0), ("LX", 5), ("RV", 1, 0), ("XT", 1),
-    ("RS", 1, 1), ("LW", 0), ("S1", 0, 0, 0), ("QT", 1, 0), ("S1", 0, 1, 0),
-    ("XC", 1, "S"), ("XT", 2), ("RV", 1, 1), ("XT", 3), ("XC", 2, "S"),
-    ("XT", 4), ("QT", 1, 1), ("XT", 5), ("XC", 3, "S"), ("LX", 6),
-    ("S1", 0, 0, 1), ("XQ", 1), ("XC", 4, "S"), ("XQ", 2), ("S1", 0, 1, 1),
-    ("LX", 7), ("E", 0, 0), ("S1", 1, 0, 0), ("S1", 1, 0, 1), ("XC", 5, "S"),
-    ("LW", 1), ("S1", 1, 1, 0), ("E", 0, 1), ("S1", 1, 1, 1), ("S1", 2, 0, 0),
-    ("E", 1, 0), ("S1", 2, 0, 1), ("S1", 2, 1, 0), ("E", 1, 1), ("S1", 2, 1, 1),
-    ("WT", 0), ("E", 2, 0), ("YT", 0), ("WC", 0, "S"), ("E", 2, 1),
-    ("WT", 1), ("YT", 1), ("YC", 0, "S"), ("XQ", 3), ("XQ", 4),
-    ("WT", 2), ("XQ", 5), ("YT", 2), ("WC", 1, "V"), ("YC", 1, "S"),
-    ("WT", 3), ("YQ", 0), ("WT", 4), ("WC", 2, "V"), ("WT", 5),
-    ("YC", 2, "S"), ("WT", 6), ("YQ", 1), ("XT", 6), ("WC", 3, "V"),
-    ("WT", 7), ("XT", 7), ("WC", 4, "S"), ("WQ", 0, 0), ("S1", 3, 0, 0),
-    ("S1", 3, 0, 1), ("WQ", 0, 1), ("WC", 5, "S"), ("S1", 3, 1, 0), ("S1", 3, 1, 1),
-    ("YQ", 2), ("WC", 6, "S"), ("S1", 4, 0, 0), ("E", 3, 0), ("S2", 0, 0),
-    ("XC", 6, "S"), ("E", 3, 1), ("S2", 1, 0), ("WC", 7, "S"), ("XQ", 6),
-    ("S2", 2, 0), ("XC", 7, "V"), ("OC", 0, 0, "S"), ("S1", 4, 0, 1), ("WQ", 1, 0),
-    ("S1", 4, 1, 0), ("OC", 1, 0, "S"), ("ST", 0, 0), ("S1", 4, 1, 1), ("S1", 5, 0, 0),
-    ("WQ", 1, 1), ("OC", 2, 0, "S"), ("ST", 1, 0), ("S1", 5, 0, 1), ("S1", 5, 1, 0),
-    ("E", 4, 0), ("S1", 5, 1, 1), ("ST", 2, 0), ("S2", 0, 1), ("E", 4, 1),
-    ("S2", 1, 1), ("E", 5, 0), ("OC", 0, 1, "S"), ("S2", 2, 1), ("E", 5, 1),
-    ("OC", 1, 1, "S"), ("ST", 0, 1), ("S1", 6, 0, 0), ("XQ", 7), ("S1", 6, 0, 1),
-    ("OC", 2, 1, "S"), ("ST", 1, 1), ("S1", 6, 1, 0), ("E", 6, 0), ("S1", 6, 1, 1),
-    ("S1", 7, 0, 0), ("ST", 2, 1), ("S1", 7, 0, 1), ("E", 6, 1), ("S1", 7, 1, 0),
-    ("S1", 7, 1, 1), ("E", 7, 0), ("YT", 3), ("E", 7, 1), ("YT", 4),
-    ("YC", 3, "S"), ("YT", 5), ("YC", 4, "V"), ("YT", 6), ("YC", 5, "S"),
-    ("YT", 7), ("YQ", 3), ("YQ", 4), ("YC", 7, "V"), ("S2", 3, 0),
-    ("YC", 6, "S"), ("S2", 3, 1), ("YQ", 5), ("OC", 3, 0, "S"), ("S2", 4, 0),
-    ("YQ", 6), ("YQ", 7), ("OC", 3, 1, "S"), ("S2", 4, 1), ("ST", 3, 0),
-    ("OC", 4, 0, "V"), ("S2", 5, 0), ("ST", 3, 1), ("OC", 4, 1, "S"), ("S2", 5, 1),
-    ("ST", 4, 0), ("OC", 5, 0, "S"), ("S2", 6, 0), ("ST", 4, 1), ("OC", 5, 1, "V"),
-    ("S2", 6, 1), ("ST", 5, 0), ("OC", 6, 0, "S"), ("S2", 7, 0), ("ST", 5, 1),
-    ("OC", 6, 1, "S"), ("S2", 7, 1), ("ST", 6, 0), ("OC", 7, 0, "V"), ("ST", 6, 1),
-    ("OC", 7, 1, "S"), ("ST", 7, 0), ("ST", 7, 1),
-]
+TILES = 8
+VCOLS = 288
 
 
 def tile_precomputedmetanet_pb_kernel(tc, transformed, coeff, task_mat, Wp, out):
@@ -65,35 +25,31 @@ def tile_precomputedmetanet_pb_kernel(tc, transformed, coeff, task_mat, Wp, out)
         psum = ctx.enter_context(tc.psum_pool(name="psum", bufs=8))
         ctx.enter_context(tc.manual_schedule())
 
-        ident_b = keep.tile([P, P], BF16, name="ident_b")
-        ident_f = keep.tile([P, P], F32, name="ident_f")
-        crow = keep.tile([P, P], BF16, name="crow")
-        c_sb = keep.tile([P, 8], F32, name="c_sb")
-        nc.vector.memset(crow[:], 0.0)
-        make_identity(nc, ident_b[:])
-        make_identity(nc, ident_f[:])
-
-        traw = keep.tile([P, 2, 4, 1024], BF16, name="traw")
+        ident = keep.tile([P, P], F32, name="ident")
+        dummy = keep.tile([P, 1], F32, name="dummy")
+        c_sb = keep.tile([P, TILES], BF16, name="c_sb")
+        traw = keep.tile([P, 2, 2, 4, 512], BF16, name="traw")
+        tgrp = keep.tile([P, 2, 2, 512, 4], BF16, name="tgrp", align_bytes=64)
         tcod = keep.tile([P, 2, 1024], U32, name="tcod", align_bytes=64)
         tscl = keep.tile([P, 2, 1024], U8, name="tscl", align_bytes=64)
         wraw = keep.tile([P, 8, 1024], BF16, name="wraw")
+        wperm = keep.tile([P, 8, 1024], BF16, name="wperm")
+        wgrp = keep.tile([P, 2, 2, 2048], BF16, name="wgrp", align_bytes=64)
         wcod = keep.tile([P, 2, 1024], U32, name="wcod", align_bytes=64)
         wscl = keep.tile([P, 2, 1024], U8, name="wscl", align_bytes=64)
-        tgrp = {}
-        for g in range(2):
-            for c in range(2):
-                tgrp[(g, c)] = keep.tile([P, 512, 4], BF16, name="tgrp%d%d" % (g, c), align_bytes=64)
-        wgrp = [keep.tile([P, 2, 2048], BF16, name="wgrp%d" % c, align_bytes=64) for c in range(2)]
-        x_sb = [keep.tile([P, 1024], BF16, name="x_sb%d" % i) for i in range(8)]
-        xgrp = [keep.tile([P, 1024], BF16, name="xgrp%d" % i, align_bytes=64) for i in range(8)]
-        xcod = [keep.tile([P, 256], U32, name="xcod%d" % i, align_bytes=64) for i in range(8)]
-        xscl = [keep.tile([P, 256], U8, name="xscl%d" % i, align_bytes=64) for i in range(8)]
-        y_sb = [keep.tile([P, 4, 256], BF16, name="y_sb%d" % i) for i in range(8)]
-        ygrp = [keep.tile([P, 1024], BF16, name="ygrp%d" % i, align_bytes=64) for i in range(8)]
-        ycod = [keep.tile([P, 256], U32, name="ycod%d" % i, align_bytes=64) for i in range(8)]
-        yscl = [keep.tile([P, 256], U8, name="yscl%d" % i, align_bytes=64) for i in range(8)]
-        obuf = [keep.tile([P, 1024], F32, name="obuf%d" % i) for i in range(8)]
+        x_sb = keep.tile([P, TILES, 1024], BF16, name="x_sb")
+        xgrp = keep.tile([P, TILES, 1024], BF16, name="xgrp", align_bytes=64)
+        xcod = keep.tile([P, TILES, 256], U32, name="xcod", align_bytes=64)
+        xscl = keep.tile([P, TILES, 256], U8, name="xscl", align_bytes=64)
+        y_sb = keep.tile([P, TILES, 1024], BF16, name="y_sb")
+        ygrp = keep.tile([P, TILES, 1024], BF16, name="ygrp", align_bytes=64)
+        ycod = keep.tile([P, TILES, 256], U32, name="ycod", align_bytes=64)
+        yscl = keep.tile([P, TILES, 256], U8, name="yscl", align_bytes=64)
+        obuf = keep.tile([P, TILES, 1024], F32, name="obuf")
         bank = {}
+
+        x_rows = transformed.rearrange("(p i) d -> p i d", i=TILES)
+        out_rows = out.rearrange("(p i) o -> p i o", i=TILES)
 
         def copy(eng, dst, src):
             if eng == "V":
@@ -101,146 +57,231 @@ def tile_precomputedmetanet_pb_kernel(tc, transformed, coeff, task_mat, Wp, out)
             else:
                 nc.scalar.copy(out=dst, in_=src)
 
-        def new_bank(key, shape, dtype):
-            t = psum.tile(shape, dtype, name="ps", tag="ps")
+        def new_bank(key, shape):
+            t = psum.tile(shape, F32, name="ps", tag="ps")
             bank[key] = t
             return t
 
-        def op_lc():
-            nc.scalar.dma_start(out=crow[0:8, :], in_=coeff.rearrange("(i p) -> i p", p=P))
-
-        def op_lt(g, u):
+        def load_t(g, c):
             rows = task_mat[512 * g : 512 * g + 512, :].rearrange("(p t) d -> p t d", t=4)
-            nc.sync.dma_start(out=traw[:, g, 2 * u : 2 * u + 2, :], in_=rows[:, 2 * u : 2 * u + 2, :])
+            nc.sync.dma_start(out=traw[:, g, c, :, :], in_=rows[:, :, 512 * c : 512 * c + 512])
 
-        def op_lx(i):
-            nc.sync.dma_start(out=x_sb[i][:], in_=transformed[P * i : P * i + P, :])
+        def load_x(i, n):
+            nc.sync.dma_start(out=x_sb[:, i : i + n, :], in_=x_rows[:, i : i + n, :])
 
-        def op_lw(c):
-            nc.sync.dma_start(
-                out=wraw[:, 4 * c : 4 * c + 4, :],
-                in_=Wp[512 * c : 512 * c + 512, :].rearrange("(j p) d -> p j d", p=P),
-            )
+        def load_w(j, n):
+            rows = Wp[P * j : P * j + P * n, :].rearrange("(j p) d -> p j d", p=P)
+            nc.sync.dma_start(out=wraw[:, j : j + n, :], in_=rows)
 
-        def op_ct():
-            t = new_bank("c", [P, P], BF16)
-            nc.tensor.transpose(t[:], crow[:], ident_b[:])
-
-        def op_cc():
-            nc.vector.tensor_copy(out=c_sb[:], in_=bank["c"][:, 0:8])
-
-        def regroup(eng, g, c, lo, hi):
-            src = traw[:, g, :, 512 * c + lo : 512 * c + hi].rearrange("p t (c i) -> p c t i", i=4)
-            dst = tgrp[(g, c)][:, lo:hi, :].rearrange("p (c i) t -> p c t i", i=4)
+        def regroup(eng, g, c):
+            lo, hi = (0, VCOLS) if eng == "V" else (VCOLS, 512)
+            src = traw[:, g, c, :, lo:hi].rearrange("p t (c i) -> p c t i", i=4)
+            dst = tgrp[:, g, c, lo:hi, :].rearrange("p (c i) t -> p c t i", i=4)
             copy(eng, dst, src)
 
-        def op_rv(g, c):
-            regroup("V", g, c, 0, VCOLS)
-
-        def op_rs(g, c):
-            regroup("S", g, c, VCOLS, 512)
-
-        def op_qt(g, c):
+        def quant_t(g, c):
             nc.vector.quantize_mx(
                 out=tcod[:, g, 512 * c : 512 * c + 512].bitcast(FP8X4),
                 scales=tscl[:, g, 512 * c : 512 * c + 512],
-                in_=tgrp[(g, c)][:].rearrange("p d t -> p (d t)"),
+                in_=tgrp[:, g, c, :, :].rearrange("p d t -> p (d t)"),
             )
 
-        def word_transposes(key, rows):
-            t = new_bank(key, [P, 4, P], F32)
+        def word_transposes(key, rows, step):
+            t = new_bank(key, [P, 4, P])
             words = rows.bitcast(F32)
             for q in range(4):
-                lo = 256 * (q // 2) + q % 2
-                nc.tensor.transpose(t[:, q, :], words[:, lo : 256 * (q // 2) + 256 : 2], ident_f[:])
+                if step == 2:
+                    lo = 256 * (q // 2)
+                    piece = words[:, lo + q % 2 : lo + 256 : 2]
+                else:
+                    piece = words[:, P * q : P * q + P]
+                nc.tensor.transpose(t[:, q, :], piece, ident[:])
 
-        def op_xt(i):
-            word_transposes(("x", i), x_sb[i][:])
+        def copy_words(key, eng, dst):
+            copy(eng, dst, bank[key][:].rearrange("p (g u) b -> p g b u", g=2))
 
-        def op_xc(i, eng):
-            dst = xgrp[i][:].bitcast(F32).rearrange("p (g b u) -> p g b u", g=2, b=P, u=2)
-            copy(eng, dst, bank[("x", i)][:].rearrange("p (g u) b -> p g b u", g=2, u=2))
+        def xt(i):
+            word_transposes(("x", i), x_sb[:, i, :], 2)
 
-        def op_xq(i):
-            nc.vector.quantize_mx(out=xcod[i][:].bitcast(FP8X4), scales=xscl[i][:], in_=xgrp[i][:])
+        def xc(i, eng):
+            copy_words(("x", i), eng, xgrp[:, i, :].bitcast(F32).rearrange("p (g b u) -> p g b u", g=2, u=2))
 
-        def op_s1(i, c, g):
-            if g == 0:
-                new_bank(("z", i, c), [P, 512], F32)
-            nc.tensor.matmul_mx(
-                out=bank[("z", i, c)][:],
-                lhsT=xcod[i][:, P * g : P * g + P].bitcast(FP8X4),
-                lhsT_scale=xscl[i][:, P * g : P * g + P],
-                rhs=tcod[:, g, 512 * c : 512 * c + 512].bitcast(FP8X4),
-                rhs_scale=tscl[:, g, 512 * c : 512 * c + 512],
-                start=(g == 0),
-                stop=(g == 1),
-            )
+        def xq(i):
+            nc.vector.quantize_mx(out=xcod[:, i, :].bitcast(FP8X4), scales=xscl[:, i, :], in_=xgrp[:, i, :])
 
-        def op_e(i, c):
-            nc.vector.scalar_tensor_tensor(
-                out=y_sb[i][:, :, 128 * c : 128 * c + 128],
-                in0=bank[("z", i, c)][:].rearrange("p (w t) -> p t w", t=4),
-                scalar=c_sb[:, i : i + 1],
-                in1=x_sb[i][:, 512 * c : 512 * c + 512].rearrange("p (w t) -> p t w", t=4),
-                op0=MULT,
-                op1=ADD,
-            )
-
-        def op_yt(i):
-            t = new_bank(("y", i), [P, 8, P], BF16)
-            for g in range(2):
-                for k in range(4):
-                    nc.tensor.transpose(t[:, 4 * g + k, :], y_sb[i][:, k, P * g : P * g + P], ident_b[:])
-
-        def op_yc(i, eng):
-            dst = ygrp[i][:].rearrange("p (g b t) -> p g b t", g=2, b=P, t=4)
-            copy(eng, dst, bank[("y", i)][:].rearrange("p (g t) b -> p g b t", g=2, t=4))
-
-        def op_yq(i):
-            nc.vector.quantize_mx(out=ycod[i][:].bitcast(FP8X4), scales=yscl[i][:], in_=ygrp[i][:])
-
-        def op_wt(j):
-            word_transposes(("w", j), wraw[:, j, :])
-
-        def op_wc(j, eng):
-            lo = P * (j % 4)
-            dst = wgrp[j // 4][:].bitcast(F32).rearrange("p g (o u) -> p g o u", u=2)[:, :, lo : lo + P, :]
-            copy(eng, dst, bank[("w", j)][:].rearrange("p (g u) o -> p g o u", g=2, u=2))
-
-        def op_wq(c, g):
-            nc.vector.quantize_mx(
-                out=wcod[:, g, 512 * c : 512 * c + 512].bitcast(FP8X4),
-                scales=wscl[:, g, 512 * c : 512 * c + 512],
-                in_=wgrp[c][:, g, :],
-            )
-
-        def op_s2(i, c):
-            t = new_bank(("o", i, c), [P, 512], F32)
+        def s1(i, c):
+            t = new_bank(("z", i, c), [P, 512])
             for g in range(2):
                 nc.tensor.matmul_mx(
                     out=t[:],
-                    lhsT=ycod[i][:, P * g : P * g + P].bitcast(FP8X4),
-                    lhsT_scale=yscl[i][:, P * g : P * g + P],
+                    lhsT=xcod[:, i, P * g : P * g + P].bitcast(FP8X4),
+                    lhsT_scale=xscl[:, i, P * g : P * g + P],
+                    rhs=tcod[:, g, 512 * c : 512 * c + 512].bitcast(FP8X4),
+                    rhs_scale=tscl[:, g, 512 * c : 512 * c + 512],
+                    start=(g == 0),
+                    stop=(g == 1),
+                )
+
+        def e(i, c):
+            z = bank[("z", i, c)][:].rearrange("p (w u e) -> p w u e", u=2, e=2)
+            x = x_sb[:, i, 512 * c : 512 * c + 512].rearrange("p (w u e) -> p w u e", u=2, e=2)
+            for u in range(2):
+                lo = 512 * c + 256 * u
+                nc.vector.scalar_tensor_tensor(
+                    out=y_sb[:, i, lo : lo + 256].rearrange("p (w e) -> p w e", e=2),
+                    in0=z[:, :, u, :],
+                    scalar=c_sb[:, i : i + 1],
+                    in1=x[:, :, u, :],
+                    op0=MULT,
+                    op1=ADD,
+                )
+
+        def yt(i):
+            word_transposes(("y", i), y_sb[:, i, :], 1)
+
+        def yc(i, eng):
+            copy_words(("y", i), eng, ygrp[:, i, :].bitcast(F32).rearrange("p (g b u) -> p g b u", g=2, u=2))
+
+        def yq(i):
+            nc.vector.quantize_mx(out=ycod[:, i, :].bitcast(FP8X4), scales=yscl[:, i, :], in_=ygrp[:, i, :])
+
+        permuted = set()
+
+        def wp(j, eng):
+            src = wraw[:, j, :].bitcast(F32).rearrange("p (g w u) -> p g u w", g=2, u=2)
+            copy(eng, wperm[:, j, :].bitcast(F32).rearrange("p (g u w) -> p g u w", g=2, u=2), src)
+            permuted.add(j)
+
+        def wt(j):
+            if j in permuted:
+                word_transposes(("w", j), wperm[:, j, :], 1)
+            else:
+                word_transposes(("w", j), wraw[:, j, :], 2)
+
+        def wc(j, eng):
+            lo = P * (j % 4)
+            dst = wgrp[:, j // 4, :, :].bitcast(F32).rearrange("p g (o u) -> p g o u", u=2)[:, :, lo : lo + P, :]
+            copy_words(("w", j), eng, dst)
+
+        def wq(c, g):
+            nc.vector.quantize_mx(
+                out=wcod[:, g, 512 * c : 512 * c + 512].bitcast(FP8X4),
+                scales=wscl[:, g, 512 * c : 512 * c + 512],
+                in_=wgrp[:, c, g, :],
+            )
+
+        def s2(i, c):
+            t = new_bank(("o", i, c), [P, 512])
+            for g in range(2):
+                nc.tensor.matmul_mx(
+                    out=t[:],
+                    lhsT=ycod[:, i, P * g : P * g + P].bitcast(FP8X4),
+                    lhsT_scale=yscl[:, i, P * g : P * g + P],
                     rhs=wcod[:, g, 512 * c : 512 * c + 512].bitcast(FP8X4),
                     rhs_scale=wscl[:, g, 512 * c : 512 * c + 512],
                     start=(g == 0),
                     stop=(g == 1),
                 )
 
-        def op_oc(i, c, eng):
-            copy(eng, obuf[i][:, 512 * c : 512 * c + 512], bank[("o", i, c)][:])
+        def oc(i, c, eng):
+            copy(eng, obuf[:, i, 512 * c : 512 * c + 512], bank[("o", i, c)][:])
 
-        def op_st(i, c):
+        def st(i, c):
             nc.sync.dma_start(
-                out=out[P * i : P * i + P, 512 * c : 512 * c + 512], in_=obuf[i][:, 512 * c : 512 * c + 512]
+                out=out_rows[:, i, 512 * c : 512 * c + 512], in_=obuf[:, i, 512 * c : 512 * c + 512]
             )
 
-        ops = {
-            "LC": op_lc, "LT": op_lt, "LX": op_lx, "LW": op_lw, "CT": op_ct, "CC": op_cc,
-            "RV": op_rv, "RS": op_rs, "QT": op_qt, "XT": op_xt, "XC": op_xc, "XQ": op_xq,
-            "S1": op_s1, "E": op_e, "YT": op_yt, "YC": op_yc, "YQ": op_yq,
-            "WT": op_wt, "WC": op_wc, "WQ": op_wq, "S2": op_s2, "OC": op_oc, "ST": op_st,
-        }
-        for step in ORDER:
-            ops[step[0]](*step[1:])
+        nc.scalar.dma_start(out=c_sb[:], in_=coeff.rearrange("(p i) -> p i", i=TILES))
+        load_t(0, 0)
+        load_x(0, 1)
+        load_t(1, 0)
+        load_x(1, 1)
+        load_t(0, 1)
+        load_x(2, 1)
+        load_t(1, 1)
+        load_x(3, 1)
+        load_w(0, 2)
+        load_x(4, 1)
+        load_w(2, 2)
+        load_x(5, 1)
+        load_w(4, 4)
+        load_x(6, 2)
+
+        nc.vector.memset(dummy[:], 0.0)
+        nc.scalar.activation(out=dummy[:], in_=dummy[:], func=COPY)
+        make_identity(nc, ident[:])
+
+        for n, (c, g) in enumerate([(0, 0), (0, 1), (1, 0), (1, 1)]):
+            regroup("V", g, c)
+            regroup("S", g, c)
+            xt(n)
+            xc(n, "S")
+            if n >= 1:
+                xq(n - 1)
+            quant_t(g, c)
+            if n >= 2:
+                s1(n - 2, 0)
+        xq(3)
+        s1(2, 0)
+        for j in range(3):
+            wt(j)
+            wc(j, "S")
+        for j in range(3, 7):
+            wp(j, "S")
+        e(0, 0)
+        e(1, 0)
+        s1(0, 1)
+        s1(1, 1)
+        e(2, 0)
+        e(0, 1)
+        s1(2, 1)
+        s1(3, 0)
+        s1(3, 1)
+        e(1, 1)
+        e(2, 1)
+        wj = 3
+        for k in range(4):
+            xt(4 + k)
+            xc(4 + k, "S")
+            if k == 0:
+                e(3, 0)
+                e(3, 1)
+            if wj < 8:
+                wt(wj)
+                wc(wj, "S")
+                wj += 1
+            xq(4 + k)
+            if k >= 1:
+                yq(k - 1)
+            yt(k)
+            yc(k, "S")
+            if wj < 8:
+                wt(wj)
+                wc(wj, "V")
+                wj += 1
+            if k == 1:
+                wq(0, 0)
+                wq(0, 1)
+        yq(3)
+        for k in range(4, 8):
+            for c in range(2):
+                s1(k, c)
+            for c in range(2):
+                e(k, c)
+            if k == 4:
+                wq(1, 0)
+                wq(1, 1)
+        for i in range(4):
+            for c in range(2):
+                s2(i, c)
+                oc(i, c, "S")
+                st(i, c)
+        for i in range(4, 8):
+            yt(i)
+            yc(i, "SV"[i % 2])
+            yq(i)
+        for i in range(4, 8):
+            for c in range(2):
+                s2(i, c)
+                oc(i, c, "SV"[c])
+                st(i, c)

@@ -191,15 +191,17 @@ def tile_precomputedmetanet_pb_kernel(tc, transformed, coeff, task_mat, Wp, out)
                 out=out_rows[:, i, 512 * c : 512 * c + 512], in_=obuf[:, i, 512 * c : 512 * c + 512]
             )
 
+        def st2(i):
+            nc.sync.dma_start(out=out_rows[:, i, :], in_=obuf[:, i, :])
+
         nc.scalar.dma_start(out=c_sb[:], in_=coeff.rearrange("(p i) -> p i", i=TILES))
         load_t(0, 0)
         load_x(0, 1)
         load_t(1, 0)
         load_x(1, 1)
+        load_x(2, 2)
         load_t(0, 1)
-        load_x(2, 1)
         load_t(1, 1)
-        load_x(3, 1)
         load_w(0, 2)
         load_x(4, 1)
         load_w(2, 2)
@@ -211,41 +213,51 @@ def tile_precomputedmetanet_pb_kernel(tc, transformed, coeff, task_mat, Wp, out)
         nc.scalar.activation(out=dummy[:], in_=dummy[:], func=COPY)
         make_identity(nc, ident[:])
 
-        for n, (c, g) in enumerate([(0, 0), (0, 1), (1, 0), (1, 1)]):
-            regroup("V", g, c)
-            regroup("S", g, c)
-            xt(n)
-            xc(n, "S")
-            if n >= 1:
-                xq(n - 1)
-            quant_t(g, c)
-            if n >= 2:
-                s1(n - 2, 0)
+        regroup("V", 0, 0)
+        regroup("S", 0, 0)
+        xt(0)
+        xc(0, "S")
+        quant_t(0, 0)
+        regroup("V", 1, 0)
+        regroup("S", 1, 0)
+        xt(1)
+        xc(1, "S")
+        xq(0)
+        quant_t(1, 0)
+        xt(2)
+        xc(2, "S")
+        xt(3)
+        xc(3, "S")
+        xq(1)
+        s1(0, 0)
+        s1(1, 0)
+        xq(2)
+        regroup("V", 0, 1)
+        regroup("S", 0, 1)
         xq(3)
         s1(2, 0)
-        for j in range(3):
+        quant_t(0, 1)
+        s1(3, 0)
+        regroup("V", 1, 1)
+        regroup("S", 1, 1)
+        e(0, 0)
+        quant_t(1, 1)
+        e(1, 0)
+        e(2, 0)
+        for j in range(2):
             wt(j)
             wc(j, "S")
-        for j in range(3, 7):
+        for j in range(2, 6):
             wp(j, "S")
-        e(0, 0)
-        e(1, 0)
-        s1(0, 1)
-        s1(1, 1)
-        e(2, 0)
-        e(0, 1)
-        s1(2, 1)
-        s1(3, 0)
-        s1(3, 1)
-        e(1, 1)
-        e(2, 1)
-        wj = 3
+        for i in range(4):
+            s1(i, 1)
+            if i == 0:
+                e(3, 0)
+            e(i, 1)
+        wj = 2
         for k in range(4):
             xt(4 + k)
             xc(4 + k, "S")
-            if k == 0:
-                e(3, 0)
-                e(3, 1)
             if wj < 8:
                 wt(wj)
                 wc(wj, "S")
@@ -262,26 +274,35 @@ def tile_precomputedmetanet_pb_kernel(tc, transformed, coeff, task_mat, Wp, out)
             if k == 1:
                 wq(0, 0)
                 wq(0, 1)
+
         yq(3)
-        for k in range(4, 8):
-            for c in range(2):
-                s1(k, c)
-            for c in range(2):
-                e(k, c)
-            if k == 4:
-                wq(1, 0)
-                wq(1, 1)
-        for i in range(4):
+        wq(1, 0)
+        wq(1, 1)
+
+        def project(i, engines="SS"):
             for c in range(2):
                 s2(i, c)
-                oc(i, c, "S")
+                oc(i, c, engines[c])
                 st(i, c)
-        for i in range(4, 8):
-            yt(i)
-            yc(i, "SV"[i % 2])
-            yq(i)
+
         for i in range(4, 8):
             for c in range(2):
-                s2(i, c)
-                oc(i, c, "SV"[c])
-                st(i, c)
+                s1(i, c)
+                e(i, c)
+            if i >= 5:
+                project(i - 5)
+        yt(4)
+        yc(4, "S")
+        yt(5)
+        yc(5, "V")
+        yq(4)
+        yq(5)
+        project(3)
+        yt(6)
+        yc(6, "S")
+        yt(7)
+        yc(7, "V")
+        yq(6)
+        yq(7)
+        for i in range(4, 8):
+            project(i, "SV")

@@ -15,7 +15,7 @@ COPY = mybir.ActivationFunctionType.Copy
 P = 128
 FLOPS = 2 * 2 * 1024 * 1024 * 1024
 TILES = 8
-VCOLS = 288
+VCOLS = 320
 
 
 def tile_precomputedmetanet_pb_kernel(tc, transformed, coeff, task_mat, Wp, out):
@@ -201,11 +201,11 @@ def tile_precomputedmetanet_pb_kernel(tc, transformed, coeff, task_mat, Wp, out)
         load_x(1, 1)
         load_x(2, 2)
         load_t(0, 1)
-        load_t(1, 1)
         load_w(0, 2)
+        load_t(1, 1)
         load_x(4, 1)
-        load_w(2, 2)
         load_x(5, 1)
+        load_w(2, 2)
         load_w(4, 4)
         load_x(6, 2)
 
@@ -226,54 +226,71 @@ def tile_precomputedmetanet_pb_kernel(tc, transformed, coeff, task_mat, Wp, out)
         quant_t(1, 0)
         xt(2)
         xc(2, "S")
-        xt(3)
-        xc(3, "S")
         xq(1)
+        xt(3)
         s1(0, 0)
         s1(1, 0)
-        xq(2)
         regroup("V", 0, 1)
         regroup("S", 0, 1)
-        xq(3)
-        s1(2, 0)
-        quant_t(0, 1)
-        s1(3, 0)
-        regroup("V", 1, 1)
-        regroup("S", 1, 1)
-        e(0, 0)
-        quant_t(1, 1)
-        e(1, 0)
-        e(2, 0)
         for j in range(2):
             wt(j)
+        xc(3, "S")
+        xq(2)
+        quant_t(0, 1)
+        s1(2, 0)
+        regroup("V", 1, 1)
+        regroup("S", 1, 1)
+        xq(3)
+        for i in (4, 5):
+            xt(i)
+        for j in range(2):
             wc(j, "S")
+        s1(3, 0)
+        for i in (4, 5):
+            xc(i, "S")
+        quant_t(1, 1)
         for j in range(2, 6):
             wp(j, "S")
+        e(0, 0)
+        e(1, 0)
+        xq(4)
+        e(2, 0)
+        e(3, 0)
+        xq(5)
         for i in range(4):
             s1(i, 1)
-            if i == 0:
-                e(3, 0)
             e(i, 1)
-        wj = 2
-        for k in range(4):
-            xt(4 + k)
-            xc(4 + k, "S")
-            if wj < 8:
-                wt(wj)
-                wc(wj, "S")
-                wj += 1
-            xq(4 + k)
-            if k >= 1:
-                yq(k - 1)
-            yt(k)
-            yc(k, "S")
-            if wj < 8:
-                wt(wj)
-                wc(wj, "V")
-                wj += 1
-            if k == 1:
-                wq(0, 0)
-                wq(0, 1)
+        wt(2)
+        wc(2, "S")
+        wt(3)
+        wc(3, "V")
+        yt(0)
+        yc(0, "S")
+        xt(6)
+        xc(6, "S")
+        wt(4)
+        wc(4, "S")
+        yq(0)
+        wq(0, 0)
+        wq(0, 1)
+        yt(1)
+        yc(1, "S")
+        xt(7)
+        xc(7, "V")
+        xq(6)
+        wt(5)
+        wc(5, "S")
+        yq(1)
+        wt(6)
+        wc(6, "S")
+        xq(7)
+        yt(2)
+        yc(2, "S")
+        wt(7)
+        wc(7, "V")
+        yt(3)
+        yc(3, "S")
+        yq(2)
 
         yq(3)
         wq(1, 0)
@@ -289,15 +306,18 @@ def tile_precomputedmetanet_pb_kernel(tc, transformed, coeff, task_mat, Wp, out)
             for c in range(2):
                 s1(i, c)
                 e(i, c)
-            if i >= 5:
-                project(i - 5)
+            if i >= 4 + 2:
+                project(i - 4 - 2)
+        for i in range(4 - 2, 2):
+            project(i)
         yt(4)
         yc(4, "S")
         yt(5)
         yc(5, "V")
         yq(4)
         yq(5)
-        project(3)
+        for i in range(2, 4):
+            project(i)
         yt(6)
         yc(6, "S")
         yt(7)

@@ -147,6 +147,18 @@ def tile_precomputedmetanet_pb_kernel(tc, transformed, coeff, task_mat, Wp, out)
 
         permuted = set()
 
+        def wp_g(j):
+            for g in range(2):
+                nc.gpsimd.tensor_scalar(
+                    out=wperm[:, j, 512 * g : 512 * g + 512].rearrange("p (u w e) -> p u w e", u=2, e=2),
+                    in0=wraw[:, j, 512 * g : 512 * g + 512].rearrange("p (w u e) -> p u w e", u=2, e=2),
+                    scalar1=1.0,
+                    scalar2=0.0,
+                    op0=MULT,
+                    op1=ADD,
+                )
+            permuted.add(j)
+
         def wp(j, eng):
             src = wraw[:, j, :].bitcast(F32).rearrange("p (g w u) -> p g u w", g=2, u=2)
             copy(eng, wperm[:, j, :].bitcast(F32).rearrange("p (g u w) -> p g u w", g=2, u=2), src)
@@ -251,6 +263,8 @@ def tile_precomputedmetanet_pb_kernel(tc, transformed, coeff, task_mat, Wp, out)
         quant_t(1, 1)
         for j in range(2, 6):
             wp(j, "S")
+        for j in (6, 7):
+            wp_g(j)
         e(0, 0)
         e(1, 0)
         xq(4)

@@ -298,15 +298,14 @@ def tile_precomputedmetanet_pb_kernel(tc, transformed, coeff, task_mat, Wp, out)
         wt(6)
         wc(6, "S")
         xq(7)
+        wt(7)
+        wc(7, "S")
         yt(2)
         yc(2, "S")
-        wt(7)
-        wc(7, "V")
         yt(3)
         yc(3, "S")
-        yq(2)
 
-        yq(3)
+
         wq(1, 0)
         wq(1, 1)
 
@@ -320,6 +319,8 @@ def tile_precomputedmetanet_pb_kernel(tc, transformed, coeff, task_mat, Wp, out)
             for c in range(2):
                 s1(i, c)
                 e(i, c)
+            if i in (4, 5):
+                yq(i - 2)
             if i >= 4 + 2:
                 project(i - 4 - 2)
         for i in range(4 - 2, 2):

@@ -70,8 +70,9 @@ def tile_precomputedmetanet_pb_kernel(tc, transformed, coeff, task_mat, Wp, out)
             nc.sync.dma_start(out=x_sb[:, i : i + n, :], in_=x_rows[:, i : i + n, :])
 
         def load_w(j, n):
-            rows = Wp[P * j : P * j + P * n, :].rearrange("(j p) d -> p j d", p=P)
-            nc.sync.dma_start(out=wraw[:, j : j + n, :], in_=rows)
+            lo = j // 4 * 512
+            rows = Wp[lo : lo + 512, :].rearrange("(p j) d -> p j d", j=4)
+            nc.sync.dma_start(out=wraw[:, j : j + n, :], in_=rows[:, j % 4 : j % 4 + n, :])
 
         def regroup(eng, g, c):
             lo, hi = (0, VCOLS) if eng == "V" else (VCOLS, 512)
@@ -196,7 +197,8 @@ def tile_precomputedmetanet_pb_kernel(tc, transformed, coeff, task_mat, Wp, out)
                 )
 
         def oc(i, c, eng):
-            copy(eng, obuf[:, i, 512 * c : 512 * c + 512], bank[("o", i, c)][:])
+            dst = obuf[:, i, 512 * c : 512 * c + 512].rearrange("p (w j) -> p w j", j=4)
+            copy(eng, dst, bank[("o", i, c)][:].rearrange("p (j w) -> p w j", j=4))
 
         def st(i, c):
             nc.sync.dma_start(
@@ -208,9 +210,8 @@ def tile_precomputedmetanet_pb_kernel(tc, transformed, coeff, task_mat, Wp, out)
 
         nc.scalar.dma_start(out=c_sb[:], in_=coeff.rearrange("(p i) -> p i", i=TILES))
         load_t(0, 0)
-        load_x(0, 1)
+        load_x(0, 2)
         load_t(1, 0)
-        load_x(1, 1)
         load_x(2, 2)
         load_t(0, 1)
         load_w(0, 2)
@@ -313,7 +314,10 @@ def tile_precomputedmetanet_pb_kernel(tc, transformed, coeff, task_mat, Wp, out)
             for c in range(2):
                 s2(i, c)
                 oc(i, c, engines[c])
-                st(i, c)
+                if i >= 4:
+                    st(i, c)
+            if i < 4:
+                st2(i)
 
         for i in range(4, 8):
             for c in range(2):

@@ -310,38 +310,40 @@ def tile_precomputedmetanet_pb_kernel(tc, transformed, coeff, task_mat, Wp, out)
         wq(1, 0)
         wq(1, 1)
 
-        def project(i, engines="SS"):
-            for c in range(2):
-                s2(i, c)
-                oc(i, c, engines[c])
-                if i >= 4:
-                    st(i, c)
-            if i < 4:
-                st2(i)
+        def project(i, c, eng="S"):
+            s2(i, c)
+            oc(i, c, eng)
+            st(i, c)
 
-        for i in range(4, 8):
+        for i in (4, 5):
             for c in range(2):
                 s1(i, c)
                 e(i, c)
-            if i in (4, 5):
-                yq(i - 2)
-            if i >= 4 + 2:
-                project(i - 4 - 2)
-        for i in range(4 - 2, 2):
-            project(i)
-        yt(4)
-        yc(4, "S")
-        yt(5)
-        yc(5, "V")
-        yq(4)
-        yq(5)
-        for i in range(2, 4):
-            project(i)
-        yt(6)
-        yc(6, "S")
-        yt(7)
-        yc(7, "V")
-        yq(6)
-        yq(7)
+            yq(i - 2)
+        project(0, 0)
+        project(1, 0)
+        for c in range(2):
+            s1(6, c)
+            e(6, c)
+        project(0, 1)
+        project(1, 1)
+        for c in range(2):
+            s1(7, c)
+            e(7, c)
+        project(2, 0, "S")
+        project(2, 1, "S")
         for i in range(4, 8):
-            project(i, "SV")
+            yt(i)
+            yc(i, "VVSS"[i - 4])
+
+        for i in range(4, 8):
+            yq(i)
+
+        for i in ():
+            yt(i)
+            yc(i, "VVSS"[i - 4])
+        for i in ():
+            yq(i)
+        for i in range(3, 8):
+            for c in range(2):
+                project(i, c, "SV"[c])

@@ -30,21 +30,21 @@ def tile_precomputedmetanet_pb_kernel(tc, transformed, coeff, task_mat, Wp, out)
         c_sb = keep.tile([P, TILES], BF16, name="c_sb")
         traw = keep.tile([P, 2, 2, 4, 512], BF16, name="traw")
         tgrp = keep.tile([P, 2, 2, 512, 4], BF16, name="tgrp", align_bytes=64)
-        tcod = keep.tile([P, 2, 1024], U32, name="tcod", align_bytes=64)
-        tscl = keep.tile([P, 2, 1024], U8, name="tscl", align_bytes=64)
+        tcod = keep.tile([P, 2, 1024], U32, name="tcod", align_bytes=256)
+        tscl = keep.tile([P, 2, 1024], U8, name="tscl", align_bytes=256)
         wraw = keep.tile([P, 8, 1024], BF16, name="wraw")
         wperm = keep.tile([P, 8, 1024], BF16, name="wperm")
         wgrp = keep.tile([P, 2, 2, 2048], BF16, name="wgrp", align_bytes=64)
-        wcod = keep.tile([P, 2, 1024], U32, name="wcod", align_bytes=64)
-        wscl = keep.tile([P, 2, 1024], U8, name="wscl", align_bytes=64)
+        wcod = keep.tile([P, 2, 1024], U32, name="wcod", align_bytes=256)
+        wscl = keep.tile([P, 2, 1024], U8, name="wscl", align_bytes=256)
         x_sb = keep.tile([P, TILES, 1024], BF16, name="x_sb")
         xgrp = keep.tile([P, TILES, 1024], BF16, name="xgrp", align_bytes=64)
-        xcod = keep.tile([P, TILES, 256], U32, name="xcod", align_bytes=64)
-        xscl = keep.tile([P, TILES, 256], U8, name="xscl", align_bytes=64)
+        xcod = keep.tile([P, TILES, 256], U32, name="xcod", align_bytes=256)
+        xscl = keep.tile([P, TILES, 256], U8, name="xscl", align_bytes=256)
         y_sb = keep.tile([P, TILES, 1024], BF16, name="y_sb")
         ygrp = keep.tile([P, TILES, 1024], BF16, name="ygrp", align_bytes=64)
-        ycod = keep.tile([P, TILES, 256], U32, name="ycod", align_bytes=64)
-        yscl = keep.tile([P, TILES, 256], U8, name="yscl", align_bytes=64)
+        ycod = keep.tile([P, TILES, 256], U32, name="ycod", align_bytes=256)
+        yscl = keep.tile([P, TILES, 256], U8, name="yscl", align_bytes=256)
         obuf = keep.tile([P, TILES, 1024], F32, name="obuf")
         bank = {}
 

from contextlib import ExitStack

import concourse.mybir as mybir
from concourse.masks import make_identity

F32 = mybir.dt.float32
BF16 = mybir.dt.bfloat16
U32 = mybir.dt.uint32
U8 = mybir.dt.uint8
FP8X4 = mybir.dt.float8_e4m3fn_x4
MULT = mybir.AluOpType.mult
ADD = mybir.AluOpType.add
COPY = mybir.ActivationFunctionType.Copy

P = 128
FLOPS = 2 * 2 * 1024 * 1024 * 1024
TILES = 8
VCOLS = 320


def tile_precomputedmetanet_pb_kernel(tc, transformed, coeff, task_mat, Wp, out):
    nc = tc.nc
    with ExitStack() as ctx:
        keep = ctx.enter_context(tc.tile_pool(name="keep", bufs=1))
        psum = ctx.enter_context(tc.psum_pool(name="psum", bufs=8))
        ctx.enter_context(tc.manual_schedule())

        ident = keep.tile([P, P], F32, name="ident")
        dummy = keep.tile([P, 1], F32, name="dummy")
        c_sb = keep.tile([P, TILES], BF16, name="c_sb")
        traw = keep.tile([P, 2, 2, 4, 512], BF16, name="traw")
        tgrp = keep.tile([P, 2, 2, 512, 4], BF16, name="tgrp", align_bytes=64)
        tcod = keep.tile([P, 2, 1024], U32, name="tcod", align_bytes=256)
        tscl = keep.tile([P, 2, 1024], U8, name="tscl", align_bytes=256)
        wraw = keep.tile([P, 8, 1024], BF16, name="wraw")
        wperm = keep.tile([P, 8, 1024], BF16, name="wperm")
        wgrp = keep.tile([P, 2, 2, 2048], BF16, name="wgrp", align_bytes=64)
        wcod = keep.tile([P, 2, 1024], U32, name="wcod", align_bytes=256)
        wscl = keep.tile([P, 2, 1024], U8, name="wscl", align_bytes=256)
        x_sb = keep.tile([P, TILES, 1024], BF16, name="x_sb")
        xgrp = keep.tile([P, TILES, 1024], BF16, name="xgrp", align_bytes=64)
        xcod = keep.tile([P, TILES, 256], U32, name="xcod", align_bytes=256)
        xscl = keep.tile([P, TILES, 256], U8, name="xscl", align_bytes=256)
        y_sb = keep.tile([P, TILES, 1024], BF16, name="y_sb")
        ygrp = keep.tile([P, TILES, 1024], BF16, name="ygrp", align_bytes=64)
        ycod = keep.tile([P, TILES, 256], U32, name="ycod", align_bytes=256)
        yscl = keep.tile([P, TILES, 256], U8, name="yscl", align_bytes=256)
        obuf = keep.tile([P, TILES, 1024], F32, name="obuf")
        bank = {}

        x_rows = transformed.rearrange("(p i) d -> p i d", i=TILES)
        out_rows = out.rearrange("(p i) o -> p i o", i=TILES)

        def copy(eng, dst, src):
            if eng == "V":
                nc.vector.tensor_copy(out=dst, in_=src)
            else:
                nc.scalar.copy(out=dst, in_=src)

        def new_bank(key, shape):
            t = psum.tile(shape, F32, name="ps", tag="ps")
            bank[key] = t
            return t

        def load_t(g, c):
            rows = task_mat[512 * g : 512 * g + 512, :].rearrange("(p t) d -> p t d", t=4)
            nc.sync.dma_start(out=traw[:, g, c, :, :], in_=rows[:, :, 512 * c : 512 * c + 512])

        def load_x(i, n):
            nc.sync.dma_start(out=x_sb[:, i : i + n, :], in_=x_rows[:, i : i + n, :])

        def load_w(j, n):
            lo = j // 4 * 512
            rows = Wp[lo : lo + 512, :].rearrange("(p j) d -> p j d", j=4)
            nc.sync.dma_start(out=wraw[:, j : j + n, :], in_=rows[:, j % 4 : j % 4 + n, :])

        def regroup(eng, g, c):
            lo, hi = (0, VCOLS) if eng == "V" else (VCOLS, 512)
            src = traw[:, g, c, :, lo:hi].rearrange("p t (c i) -> p c t i", i=4)
            dst = tgrp[:, g, c, lo:hi, :].rearrange("p (c i) t -> p c t i", i=4)
            copy(eng, dst, src)

        def quant_t(g, c):
            nc.vector.quantize_mx(
                out=tcod[:, g, 512 * c : 512 * c + 512].bitcast(FP8X4),
                scales=tscl[:, g, 512 * c : 512 * c + 512],
                in_=tgrp[:, g, c, :, :].rearrange("p d t -> p (d t)"),
            )

        def word_transposes(key, rows, step):
            t = new_bank(key, [P, 4, P])
            words = rows.bitcast(F32)
            for q in range(4):
                if step == 2:
                    lo = 256 * (q // 2)
                    piece = words[:, lo + q % 2 : lo + 256 : 2]
                else:
                    piece = words[:, P * q : P * q + P]
                nc.tensor.transpose(t[:, q, :], piece, ident[:])

        def copy_words(key, eng, dst):
            copy(eng, dst, bank[key][:].rearrange("p (g u) b -> p g b u", g=2))

        def xt(i):
            word_transposes(("x", i), x_sb[:, i, :], 2)

        def xc(i, eng):
            copy_words(("x", i), eng, xgrp[:, i, :].bitcast(F32).rearrange("p (g b u) -> p g b u", g=2, u=2))

        def xq(i):
            nc.vector.quantize_mx(out=xcod[:, i, :].bitcast(FP8X4), scales=xscl[:, i, :], in_=xgrp[:, i, :])

        def s1(i, c):
            t = new_bank(("z", i, c), [P, 512])
            for g in range(2):
                nc.tensor.matmul_mx(
                    out=t[:],
                    lhsT=xcod[:, i, P * g : P * g + P].bitcast(FP8X4),
                    lhsT_scale=xscl[:, i, P * g : P * g + P],
                    rhs=tcod[:, g, 512 * c : 512 * c + 512].bitcast(FP8X4),
                    rhs_scale=tscl[:, g, 512 * c : 512 * c + 512],
                    start=(g == 0),
                    stop=(g == 1),
                )

        def e(i, c):
            z = bank[("z", i, c)][:].rearrange("p (w u e) -> p w u e", u=2, e=2)
            x = x_sb[:, i, 512 * c : 512 * c + 512].rearrange("p (w u e) -> p w u e", u=2, e=2)
            for u in range(2):
                lo = 512 * c + 256 * u
                nc.vector.scalar_tensor_tensor(
                    out=y_sb[:, i, lo : lo + 256].rearrange("p (w e) -> p w e", e=2),
                    in0=z[:, :, u, :],
                    scalar=c_sb[:, i : i + 1],
                    in1=x[:, :, u, :],
                    op0=MULT,
                    op1=ADD,
                )

        def yt(i):
            word_transposes(("y", i), y_sb[:, i, :], 1)

        def yc(i, eng):
            copy_words(("y", i), eng, ygrp[:, i, :].bitcast(F32).rearrange("p (g b u) -> p g b u", g=2, u=2))

        def yq(i):
            nc.vector.quantize_mx(out=ycod[:, i, :].bitcast(FP8X4), scales=yscl[:, i, :], in_=ygrp[:, i, :])

        permuted = set()

        def wp_g(j):
            for g in range(2):
                nc.gpsimd.tensor_scalar(
                    out=wperm[:, j, 512 * g : 512 * g + 512].rearrange("p (u w e) -> p u w e", u=2, e=2),
                    in0=wraw[:, j, 512 * g : 512 * g + 512].rearrange("p (w u e) -> p u w e", u=2, e=2),
                    scalar1=1.0,
                    scalar2=0.0,
                    op0=MULT,
                    op1=ADD,
                )
            permuted.add(j)

        def wp(j, eng):
            src = wraw[:, j, :].bitcast(F32).rearrange("p (g w u) -> p g u w", g=2, u=2)
            copy(eng, wperm[:, j, :].bitcast(F32).rearrange("p (g u w) -> p g u w", g=2, u=2), src)
            permuted.add(j)

        def wt(j):
            if j in permuted:
                word_transposes(("w", j), wperm[:, j, :], 1)
            else:
                word_transposes(("w", j), wraw[:, j, :], 2)

        def wc(j, eng):
            lo = P * (j % 4)
            dst = wgrp[:, j // 4, :, :].bitcast(F32).rearrange("p g (o u) -> p g o u", u=2)[:, :, lo : lo + P, :]
            copy_words(("w", j), eng, dst)

        def wq(c, g):
            nc.vector.quantize_mx(
                out=wcod[:, g, 512 * c : 512 * c + 512].bitcast(FP8X4),
                scales=wscl[:, g, 512 * c : 512 * c + 512],
                in_=wgrp[:, c, g, :],
            )

        def s2(i, c):
            t = new_bank(("o", i, c), [P, 512])
            for g in range(2):
                nc.tensor.matmul_mx(
                    out=t[:],
                    lhsT=ycod[:, i, P * g : P * g + P].bitcast(FP8X4),
                    lhsT_scale=yscl[:, i, P * g : P * g + P],
                    rhs=wcod[:, g, 512 * c : 512 * c + 512].bitcast(FP8X4),
                    rhs_scale=wscl[:, g, 512 * c : 512 * c + 512],
                    start=(g == 0),
                    stop=(g == 1),
                )

        def oc(i, c, eng):
            dst = obuf[:, i, 512 * c : 512 * c + 512].rearrange("p (w j) -> p w j", j=4)
            copy(eng, dst, bank[("o", i, c)][:].rearrange("p (j w) -> p w j", j=4))

        def st(i, c):
            nc.sync.dma_start(
                out=out_rows[:, i, 512 * c : 512 * c + 512], in_=obuf[:, i, 512 * c : 512 * c + 512]
            )

        def st2(i):
            nc.sync.dma_start(out=out_rows[:, i, :], in_=obuf[:, i, :])

        nc.scalar.dma_start(out=c_sb[:], in_=coeff.rearrange("(p i) -> p i", i=TILES))
        load_t(0, 0)
        load_x(0, 2)
        load_t(1, 0)
        load_x(2, 2)
        load_t(0, 1)
        load_w(0, 2)
        load_t(1, 1)
        load_x(4, 1)
        load_x(5, 1)
        load_w(2, 2)
        load_w(4, 4)
        load_x(6, 2)

        nc.vector.memset(dummy[:], 0.0)
        nc.scalar.activation(out=dummy[:], in_=dummy[:], func=COPY)
        make_identity(nc, ident[:])

        regroup("V", 0, 0)
        regroup("S", 0, 0)
        xt(0)
        xc(0, "S")
        quant_t(0, 0)
        regroup("V", 1, 0)
        regroup("S", 1, 0)
        xt(1)
        xc(1, "S")
        xq(0)
        quant_t(1, 0)
        xt(2)
        xc(2, "S")
        xq(1)
        xt(3)
        s1(0, 0)
        s1(1, 0)
        regroup("V", 0, 1)
        regroup("S", 0, 1)
        for j in range(2):
            wt(j)
        xc(3, "S")
        xq(2)
        quant_t(0, 1)
        s1(2, 0)
        regroup("V", 1, 1)
        regroup("S", 1, 1)
        xq(3)
        for i in (4, 5):
            xt(i)
        for j in range(2):
            wc(j, "S")
        s1(3, 0)
        for i in (4, 5):
            xc(i, "S")
        quant_t(1, 1)
        for j in range(2, 6):
            wp(j, "S")
        for j in (6, 7):
            wp_g(j)
        e(0, 0)
        e(1, 0)
        xq(4)
        e(2, 0)
        e(3, 0)
        xq(5)
        for i in range(4):
            s1(i, 1)
            e(i, 1)
        wt(2)
        wc(2, "S")
        wt(3)
        wc(3, "V")
        yt(0)
        yc(0, "S")
        xt(6)
        xc(6, "S")
        wt(4)
        wc(4, "S")
        yq(0)
        wq(0, 0)
        wq(0, 1)
        yt(1)
        yc(1, "S")
        xt(7)
        xc(7, "V")
        xq(6)
        wt(5)
        wc(5, "S")
        yq(1)
        wt(6)
        wc(6, "S")
        xq(7)
        wt(7)
        wc(7, "S")
        yt(2)
        yc(2, "S")
        yt(3)
        yc(3, "S")


        wq(1, 0)
        wq(1, 1)

        def project(i, c, eng="S"):
            s2(i, c)
            oc(i, c, eng)
            st(i, c)

        for i in (4, 5):
            for c in range(2):
                s1(i, c)
                e(i, c)
            yq(i - 2)
        project(0, 0)
        project(1, 0)
        for c in range(2):
            s1(6, c)
            e(6, c)
        project(0, 1)
        project(1, 1)
        for c in range(2):
            s1(7, c)
            e(7, c)
        project(2, 0, "S")
        project(2, 1, "S")
        for i in range(4, 8):
            yt(i)
            yc(i, "VVSS"[i - 4])

        for i in range(4, 8):
            yq(i)

        for i in ():
            yt(i)
            yc(i, "VVSS"[i - 4])
        for i in ():
            yq(i)
        for i in range(3, 8):
            for c in range(2):
                project(i, c, "SV"[c])
